import numpy as np
import ml_dtypes

BF16 = ml_dtypes.bfloat16


def bf(x):
    return np.asarray(x, np.float32).astype(BF16)


def f32(x):
    return np.asarray(x, np.float32)


def f64(x):
    return np.asarray(x).astype(np.float64)


def striped(idx):
    return np.tile(idx.reshape(-1, 16).T, (8, 1))


C, S, B, T, N = 1024, 1024, 4, 512, 2048
EPS = 1e-6


def setup_inputs():
    return {"tok_emb": f32(np.random.standard_normal((C, S))), "pos_emb": f32(np.random.standard_normal((C, T))), "norm_w": f32(1.0 + 0.1 * np.random.standard_normal((C, 1))), "head": bf(np.random.standard_normal((C, S)) / np.sqrt(C)), "offs": striped(np.concatenate([np.random.permutation(S)[:T] for _ in range(B)]))}


def reference(tok_emb, pos_emb, norm_w, head, offs):
    idx = offs[:16].T.reshape(-1)
    out = np.zeros((S, N), np.float64)
    for b in range(B):
        cols = slice(b * T, (b + 1) * T)
        h = f64(tok_emb)[:, idx[cols]] + f64(pos_emb)
        r = 1.0 / np.sqrt(np.mean(h * h, axis=0, keepdims=True) + EPS)
        y = f64(norm_w) * (h * r)
        out[:, cols] = f64(head).T @ y
    return out

@@ -1,0 +1,80 @@
+import concourse.mybir as mybir
+
+F32 = mybir.dt.float32
+BF16 = mybir.dt.bfloat16
+U16 = mybir.dt.uint16
+ADD = mybir.AluOpType.add
+MULT = mybir.AluOpType.mult
+ACT = mybir.ActivationFunctionType
+
+P = 128
+C, S, B, T = 1024, 1024, 4, 512
+CB = C // P
+VB = S // P
+EPS = 1e-6
+FLOPS = 2 * C * S * B * T
+
+
+def tile_bitnet_b_kernel(tc, tok_emb, pos_emb, norm_w, head, offs, out):
+    nc = tc.nc
+
+    tok_blocks = tok_emb.rearrange("(p a) s -> a p s", a=CB)
+    pos_blocks = pos_emb.rearrange("(p a) t -> a p t", a=CB)
+    head_blocks = head.rearrange("(p a) v -> a p v", a=CB)
+
+    with (
+        tc.tile_pool(name="held", bufs=1) as held,
+        tc.tile_pool(name="hidden", bufs=4) as hidden,
+        tc.tile_pool(name="operands", bufs=2) as operands,
+        tc.tile_pool(name="results", bufs=4) as results,
+        tc.psum_pool(name="sums", bufs=2) as sums,
+        tc.psum_pool(name="products", bufs=6) as products,
+    ):
+        offsets = held.tile([P, B * T // 16], U16, name="offsets")
+        nc.sync.dma_start(offsets[:], offs)
+        gain = held.tile([P, CB], F32, name="gain")
+        nc.scalar.dma_start(gain[:], norm_w.rearrange("(p a) o -> p (a o)", a=CB))
+
+        tok = [held.tile([P, S], F32, name="tok%d" % a) for a in range(CB)]
+        pos = held.tile([P, CB, T], F32, name="pos")
+        head_sb = held.tile([P, CB, S], BF16, name="head_sb")
+        for a in range(CB):
+            nc.sync.dma_start(tok[a][:], tok_blocks[a])
+            nc.sync.dma_start(pos[:, a, :], pos_blocks[a])
+        for a in range(CB):
+            nc.sync.dma_start(head_sb[:, a, :], head_blocks[a])
+
+        ones = held.tile([P, P], BF16, name="ones")
+        nc.vector.memset(ones[:], 1.0)
+        eps = held.tile([P, 1], F32, name="eps")
+        nc.vector.memset(eps[:], EPS)
+
+        for b in range(B):
+            piece = offsets[:, b * (T // 16) : (b + 1) * (T // 16)]
+            squares = operands.tile([P, CB, T], BF16, name="squares")
+            scaled = operands.tile([P, CB, T], BF16, name="scaled")
+            for a in range(CB):
+                h = hidden.tile([P, T], F32, name="h")
+                nc.vector.tensor_tensor(h[:], tok[a][:].indirect(piece), pos[:, a, :], ADD)
+                nc.scalar.activation(squares[:, a, :], h[:], ACT.Square)
+                nc.scalar.activation(scaled[:, a, :], h[:], ACT.Identity, scale=gain[:, a : a + 1])
+
+            total = sums.tile([P, T], F32, name="total")
+            for a in range(CB):
+                nc.tensor.matmul(total[:], ones[:], squares[:, a, :], start=(a == 0), stop=(a == CB - 1))
+            r = results.tile([P, T], F32, name="r")
+            nc.scalar.activation(r[:], total[:], ACT.Abs_reciprocal_sqrt, bias=eps[:], scale=1.0 / C)
+
+            for v in range(VB):
+                product = products.tile([P, T], F32, name="product")
+                for a in range(CB):
+                    nc.tensor.matmul(
+                        product[:],
+                        head_sb[:, a, v * P : (v + 1) * P],
+                        scaled[:, a, :],
+                        start=(a == 0),
+                        stop=(a == CB - 1),
+                    )
+                logits = results.tile([P, T], F32, name="logits")
+                nc.vector.tensor_tensor(logits[:], product[:], r[:], MULT)
+                nc.sync.dma_start(out[v * P : (v + 1) * P, b * T : (b + 1) * T], logits[:])

@@ -15,6 +15,11 @@ EPS = 1e-6
 FLOPS = 2 * C * S * B * T
 
 
+AT_START = 2
+BANKS = 7
+FOLDED_FROM = 1
+
+
 def tile_bitnet_b_kernel(tc, tok_emb, pos_emb, norm_w, head, offs, out):
     nc = tc.nc
 
@@ -26,9 +31,9 @@ def tile_bitnet_b_kernel(tc, tok_emb, pos_emb, norm_w, head, offs, out):
         tc.tile_pool(name="held", bufs=1) as held,
         tc.tile_pool(name="hidden", bufs=4) as hidden,
         tc.tile_pool(name="operands", bufs=2) as operands,
-        tc.tile_pool(name="results", bufs=4) as results,
-        tc.psum_pool(name="sums", bufs=2) as sums,
-        tc.psum_pool(name="products", bufs=6) as products,
+        tc.tile_pool(name="results", bufs=8) as results,
+        tc.psum_pool(name="sums", bufs=1) as sums,
+        tc.psum_pool(name="products", bufs=BANKS) as products,
     ):
         offsets = held.tile([P, B * T // 16], U16, name="offsets")
         nc.sync.dma_start(offsets[:], offs)
@@ -41,7 +46,6 @@ def tile_bitnet_b_kernel(tc, tok_emb, pos_emb, norm_w, head, offs, out):
         for a in range(CB):
             nc.sync.dma_start(tok[a][:], tok_blocks[a])
             nc.sync.dma_start(pos[:, a, :], pos_blocks[a])
-        for a in range(CB):
             nc.sync.dma_start(head_sb[:, a, :], head_blocks[a])
 
         ones = held.tile([P, P], BF16, name="ones")
@@ -49,32 +53,60 @@ def tile_bitnet_b_kernel(tc, tok_emb, pos_emb, norm_w, head, offs, out):
         eps = held.tile([P, 1], F32, name="eps")
         nc.vector.memset(eps[:], EPS)
 
-        for b in range(B):
+        squares = {}
+        scaled = {}
+
+        def prepare(b, a):
+            if a == 0:
+                squares[b] = operands.tile([P, CB, T], BF16, name="squares")
+                scaled[b] = operands.tile([P, CB, T], BF16, name="scaled")
             piece = offsets[:, b * (T // 16) : (b + 1) * (T // 16)]
-            squares = operands.tile([P, CB, T], BF16, name="squares")
-            scaled = operands.tile([P, CB, T], BF16, name="scaled")
-            for a in range(CB):
-                h = hidden.tile([P, T], F32, name="h")
-                nc.vector.tensor_tensor(h[:], tok[a][:].indirect(piece), pos[:, a, :], ADD)
-                nc.scalar.activation(squares[:, a, :], h[:], ACT.Square)
-                nc.scalar.activation(scaled[:, a, :], h[:], ACT.Identity, scale=gain[:, a : a + 1])
+            h = hidden.tile([P, T], F32, name="h")
+            nc.vector.tensor_tensor(h[:], tok[a][:].indirect(piece), pos[:, a, :], ADD)
+            nc.scalar.activation(scaled[b][:, a, :], h[:], ACT.Identity, scale=gain[:, a : a + 1])
+            nc.scalar.activation(squares[b][:, a, :], h[:], ACT.Square)
 
+        r = {}
+
+        def norm(b):
+            parts = CB
+            while b >= FOLDED_FROM and parts > 1:
+                parts //= 2
+                lower = squares[b][:, 0:parts, :]
+                nc.vector.tensor_tensor(lower, lower, squares[b][:, parts : 2 * parts, :], ADD)
             total = sums.tile([P, T], F32, name="total")
-            for a in range(CB):
-                nc.tensor.matmul(total[:], ones[:], squares[:, a, :], start=(a == 0), stop=(a == CB - 1))
-            r = results.tile([P, T], F32, name="r")
-            nc.scalar.activation(r[:], total[:], ACT.Abs_reciprocal_sqrt, bias=eps[:], scale=1.0 / C)
+            for a in range(parts):
+                nc.tensor.matmul(total[:], ones[:], squares[b][:, a, :], start=(a == 0), stop=(a == parts - 1))
+            r[b] = results.tile([P, T], F32, name="r", bufs=2)
+            nc.scalar.activation(r[b][:], total[:], ACT.Abs_reciprocal_sqrt, bias=eps[:], scale=1.0 / C)
 
-            for v in range(VB):
-                product = products.tile([P, T], F32, name="product")
-                for a in range(CB):
+        def logits_of(b, words):
+            product = {v: products.tile([P, T], F32, name="product") for v in words}
+            for a in range(CB):
+                for v in words:
                     nc.tensor.matmul(
-                        product[:],
+                        product[v][:],
                         head_sb[:, a, v * P : (v + 1) * P],
-                        scaled[:, a, :],
+                        scaled[b][:, a, :],
                         start=(a == 0),
                         stop=(a == CB - 1),
                     )
+            for v in words:
                 logits = results.tile([P, T], F32, name="logits")
-                nc.vector.tensor_tensor(logits[:], product[:], r[:], MULT)
+                nc.vector.tensor_tensor(logits[:], product[v][:], r[b][:], MULT)
                 nc.sync.dma_start(out[v * P : (v + 1) * P, b * T : (b + 1) * T], logits[:])
+
+        for a in range(CB):
+            for b in range(AT_START):
+                prepare(b, a)
+        norm(0)
+        logits_of(0, range(BANKS))
+        for v in range(BANKS, VB):
+            logits_of(0, [v])
+
+        for b in range(1, B):
+            norm(b)
+            for v in range(VB):
+                logits_of(b, [v])
+                if AT_START <= b + 1 < B:
+                    prepare(b + 1, v)

@@ -14,10 +14,10 @@ VB = S // P
 EPS = 1e-6
 FLOPS = 2 * C * S * B * T
 
-
-AT_START = 2
 BANKS = 7
-FOLDED_FROM = 1
+BEHIND = 2
+AT_ONCE = 4
+ADD_UP_AFTER = 2
 
 
 def tile_bitnet_b_kernel(tc, tok_emb, pos_emb, norm_w, head, offs, out):
@@ -29,9 +29,8 @@ def tile_bitnet_b_kernel(tc, tok_emb, pos_emb, norm_w, head, offs, out):
 
     with (
         tc.tile_pool(name="held", bufs=1) as held,
-        tc.tile_pool(name="hidden", bufs=4) as hidden,
         tc.tile_pool(name="operands", bufs=2) as operands,
-        tc.tile_pool(name="results", bufs=8) as results,
+        tc.tile_pool(name="results", bufs=12) as results,
         tc.psum_pool(name="sums", bufs=1) as sums,
         tc.psum_pool(name="products", bufs=BANKS) as products,
     ):
@@ -52,36 +51,41 @@ def tile_bitnet_b_kernel(tc, tok_emb, pos_emb, norm_w, head, offs, out):
         nc.vector.memset(ones[:], 1.0)
         eps = held.tile([P, 1], F32, name="eps")
         nc.vector.memset(eps[:], EPS)
+        warm = held.tile([P, 1], F32, name="warm")
+        nc.scalar.activation(warm[:], eps[:], ACT.Abs_reciprocal_sqrt)
 
         squares = {}
         scaled = {}
+        r = {}
+        product = {}
 
         def prepare(b, a):
             if a == 0:
                 squares[b] = operands.tile([P, CB, T], BF16, name="squares")
                 scaled[b] = operands.tile([P, CB, T], BF16, name="scaled")
             piece = offsets[:, b * (T // 16) : (b + 1) * (T // 16)]
-            h = hidden.tile([P, T], F32, name="h")
+            h = results.tile([P, T], F32, name="h", tag="from_vector")
             nc.vector.tensor_tensor(h[:], tok[a][:].indirect(piece), pos[:, a, :], ADD)
             nc.scalar.activation(scaled[b][:, a, :], h[:], ACT.Identity, scale=gain[:, a : a + 1])
             nc.scalar.activation(squares[b][:, a, :], h[:], ACT.Square)
 
-        r = {}
-
-        def norm(b):
+        def add_up(b):
             parts = CB
-            while b >= FOLDED_FROM and parts > 1:
+            while parts > 1:
                 parts //= 2
                 lower = squares[b][:, 0:parts, :]
                 nc.vector.tensor_tensor(lower, lower, squares[b][:, parts : 2 * parts, :], ADD)
+
+        def norm(b, parts):
             total = sums.tile([P, T], F32, name="total")
             for a in range(parts):
                 nc.tensor.matmul(total[:], ones[:], squares[b][:, a, :], start=(a == 0), stop=(a == parts - 1))
             r[b] = results.tile([P, T], F32, name="r", bufs=2)
             nc.scalar.activation(r[b][:], total[:], ACT.Abs_reciprocal_sqrt, bias=eps[:], scale=1.0 / C)
 
-        def logits_of(b, words):
-            product = {v: products.tile([P, T], F32, name="product") for v in words}
+        def multiply(b, words):
+            for v in words:
+                product[v] = products.tile([P, T], F32, name="product")
             for a in range(CB):
                 for v in words:
                     nc.tensor.matmul(
@@ -91,22 +95,30 @@ def tile_bitnet_b_kernel(tc, tok_emb, pos_emb, norm_w, head, offs, out):
                         start=(a == 0),
                         stop=(a == CB - 1),
                     )
-            for v in words:
-                logits = results.tile([P, T], F32, name="logits")
-                nc.vector.tensor_tensor(logits[:], product[v][:], r[b][:], MULT)
-                nc.sync.dma_start(out[v * P : (v + 1) * P, b * T : (b + 1) * T], logits[:])
+
+        def store(b, v):
+            logits = results.tile([P, T], F32, name="logits", tag="from_vector")
+            nc.vector.tensor_tensor(logits[:], product[v][:], r[b][:], MULT)
+            nc.sync.dma_start(out[v * P : (v + 1) * P, b * T : (b + 1) * T], logits[:])
 
         for a in range(CB):
-            for b in range(AT_START):
-                prepare(b, a)
-        norm(0)
-        logits_of(0, range(BANKS))
-        for v in range(BANKS, VB):
-            logits_of(0, [v])
+            prepare(0, a)
+            if a < CB - BEHIND:
+                prepare(1, a)
+        norm(0, CB)
+        for a in range(CB - BEHIND, CB):
+            prepare(1, a)
+        multiply(0, range(BANKS))
 
-        for b in range(1, B):
-            norm(b)
+        for b in range(B):
             for v in range(VB):
-                logits_of(b, [v])
-                if AT_START <= b + 1 < B:
-                    prepare(b + 1, v)
+                if 1 <= b < B - 1 and v < CB // AT_ONCE:
+                    for a in range(AT_ONCE * v, AT_ONCE * (v + 1)):
+                        prepare(b + 1, a)
+                if b > 0 or v >= BANKS:
+                    multiply(b, [v])
+                store(b, v)
+                if b + 1 < B and v == ADD_UP_AFTER:
+                    add_up(b + 1)
+            if b + 1 < B:
+                norm(b + 1, 1)

@@ -15,7 +15,7 @@ EPS = 1e-6
 FLOPS = 2 * C * S * B * T
 
 BANKS = 7
-BEHIND = 2
+SKIP_EVERY = 4
 AT_ONCE = 4
 ADD_UP_AFTER = 2
 
@@ -83,30 +83,35 @@ def tile_bitnet_b_kernel(tc, tok_emb, pos_emb, norm_w, head, offs, out):
             r[b] = results.tile([P, T], F32, name="r", bufs=2)
             nc.scalar.activation(r[b][:], total[:], ACT.Abs_reciprocal_sqrt, bias=eps[:], scale=1.0 / C)
 
-        def multiply(b, words):
+        def multiply(b, words, lo=0, hi=T):
             for v in words:
-                product[v] = products.tile([P, T], F32, name="product")
+                product[v] = products.tile([P, hi - lo], F32, name="product")
             for a in range(CB):
                 for v in words:
                     nc.tensor.matmul(
                         product[v][:],
                         head_sb[:, a, v * P : (v + 1) * P],
-                        scaled[b][:, a, :],
+                        scaled[b][:, a, lo:hi],
                         start=(a == 0),
                         stop=(a == CB - 1),
                     )
 
-        def store(b, v):
-            logits = results.tile([P, T], F32, name="logits", tag="from_vector")
-            nc.vector.tensor_tensor(logits[:], product[v][:], r[b][:], MULT)
-            nc.sync.dma_start(out[v * P : (v + 1) * P, b * T : (b + 1) * T], logits[:])
+        def store(b, v, lo=0, hi=T):
+            source = product[v]
+            if b == 0 and v == 0:
+                source = results.tile([P, hi - lo], F32, name="moved", tag="from_vector")
+                nc.vector.tensor_copy(source[:], product[v][:])
+            logits = results.tile([P, hi - lo], F32, name="logits", tag="from_vector")
+            nc.vector.tensor_tensor(logits[:], source[:], r[b][:, lo:hi], MULT)
+            nc.sync.dma_start(out[v * P : (v + 1) * P, b * T + lo : b * T + hi], logits[:])
 
+        turns = [a for a in range(CB) if a % SKIP_EVERY != SKIP_EVERY - 1]
         for a in range(CB):
             prepare(0, a)
-            if a < CB - BEHIND:
-                prepare(1, a)
+            if a in turns:
+                prepare(1, turns.index(a))
         norm(0, CB)
-        for a in range(CB - BEHIND, CB):
+        for a in range(len(turns), CB):
             prepare(1, a)
         multiply(0, range(BANKS))
 
@@ -115,10 +120,16 @@ def tile_bitnet_b_kernel(tc, tok_emb, pos_emb, norm_w, head, offs, out):
                 if 1 <= b < B - 1 and v < CB // AT_ONCE:
                     for a in range(AT_ONCE * v, AT_ONCE * (v + 1)):
                         prepare(b + 1, a)
+                if b == B - 1 and v == VB - 1:
+                    multiply(b, [v], 0, T // 2)
+                    store(b, v, 0, T // 2)
+                    multiply(b, [v], T // 2, T)
+                    store(b, v, T // 2, T)
+                    continue
                 if b > 0 or v >= BANKS:
                     multiply(b, [v])
+                if b > 0 and v == 0:
+                    norm(b, 1)
                 store(b, v)
                 if b + 1 < B and v == ADD_UP_AFTER:
                     add_up(b + 1)
-            if b + 1 < B:
-                norm(b + 1, 1)

@@ -15,7 +15,6 @@ EPS = 1e-6
 FLOPS = 2 * C * S * B * T
 
 BANKS = 7
-SKIP_EVERY = 4
 AT_ONCE = 4
 ADD_UP_AFTER = 2
 
@@ -105,14 +104,10 @@ def tile_bitnet_b_kernel(tc, tok_emb, pos_emb, norm_w, head, offs, out):
             nc.vector.tensor_tensor(logits[:], source[:], r[b][:, lo:hi], MULT)
             nc.sync.dma_start(out[v * P : (v + 1) * P, b * T + lo : b * T + hi], logits[:])
 
-        turns = [a for a in range(CB) if a % SKIP_EVERY != SKIP_EVERY - 1]
         for a in range(CB):
             prepare(0, a)
-            if a in turns:
-                prepare(1, turns.index(a))
-        norm(0, CB)
-        for a in range(len(turns), CB):
             prepare(1, a)
+        norm(0, CB)
         multiply(0, range(BANKS))
 
         for b in range(B):

@@ -17,6 +17,8 @@ FLOPS = 2 * C * S * B * T
 BANKS = 7
 AT_ONCE = 4
 ADD_UP_AFTER = 2
+NORM_AFTER = 1
+FINISH_AT_ONCE = 2
 
 
 def tile_bitnet_b_kernel(tc, tok_emb, pos_emb, norm_w, head, offs, out):
@@ -57,10 +59,14 @@ def tile_bitnet_b_kernel(tc, tok_emb, pos_emb, norm_w, head, offs, out):
         scaled = {}
         r = {}
         product = {}
+        parked = {}
 
         def prepare(b, a):
             if a == 0:
-                squares[b] = operands.tile([P, CB, T], BF16, name="squares")
+                if b == 0:
+                    squares[b] = held.tile([P, CB, T], BF16, name="squares_kept")
+                else:
+                    squares[b] = operands.tile([P, CB, T], BF16, name="squares")
                 scaled[b] = operands.tile([P, CB, T], BF16, name="scaled")
             piece = offsets[:, b * (T // 16) : (b + 1) * (T // 16)]
             h = results.tile([P, T], F32, name="h", tag="from_vector")
@@ -75,16 +81,18 @@ def tile_bitnet_b_kernel(tc, tok_emb, pos_emb, norm_w, head, offs, out):
                 lower = squares[b][:, 0:parts, :]
                 nc.vector.tensor_tensor(lower, lower, squares[b][:, parts : 2 * parts, :], ADD)
 
-        def norm(b, parts):
+        def norm(b):
             total = sums.tile([P, T], F32, name="total")
-            for a in range(parts):
-                nc.tensor.matmul(total[:], ones[:], squares[b][:, a, :], start=(a == 0), stop=(a == parts - 1))
-            r[b] = results.tile([P, T], F32, name="r", bufs=2)
+            nc.tensor.matmul(total[:], ones[:], squares[b][:, 0, :], start=True, stop=True)
+            r[b] = held.tile([P, T], F32, name="r%d" % b)
             nc.scalar.activation(r[b][:], total[:], ACT.Abs_reciprocal_sqrt, bias=eps[:], scale=1.0 / C)
 
         def multiply(b, words, lo=0, hi=T):
             for v in words:
-                product[v] = products.tile([P, hi - lo], F32, name="product")
+                if v < BANKS or b > 0:
+                    product[v] = products.tile([P, hi - lo], F32, name="product")
+                else:
+                    product[v] = sums.tile([P, hi - lo], F32, name="total")
             for a in range(CB):
                 for v in words:
                     nc.tensor.matmul(
@@ -95,11 +103,15 @@ def tile_bitnet_b_kernel(tc, tok_emb, pos_emb, norm_w, head, offs, out):
                         stop=(a == CB - 1),
                     )
 
-        def store(b, v, lo=0, hi=T):
-            source = product[v]
-            if b == 0 and v == 0:
-                source = results.tile([P, hi - lo], F32, name="moved", tag="from_vector")
-                nc.vector.tensor_copy(source[:], product[v][:])
+        def park(v):
+            if v == 0:
+                parked[v] = results.tile([P, T], F32, name="moved", tag="from_vector")
+                nc.vector.tensor_copy(parked[v][:], product[v][:])
+            else:
+                parked[v] = held.tile([P, T], F32, name="parked%d" % v)
+                nc.scalar.copy(parked[v][:], product[v][:])
+
+        def store(b, v, source, lo=0, hi=T):
             logits = results.tile([P, hi - lo], F32, name="logits", tag="from_vector")
             nc.vector.tensor_tensor(logits[:], source[:], r[b][:, lo:hi], MULT)
             nc.sync.dma_start(out[v * P : (v + 1) * P, b * T + lo : b * T + hi], logits[:])
@@ -107,24 +119,37 @@ def tile_bitnet_b_kernel(tc, tok_emb, pos_emb, norm_w, head, offs, out):
         for a in range(CB):
             prepare(0, a)
             prepare(1, a)
-        norm(0, CB)
-        multiply(0, range(BANKS))
+        multiply(0, range(VB))
 
-        for b in range(B):
+        for v in [0, VB - 1] + list(range(1, VB - 1)):
+            park(v)
+        add_up(1)
+
+        for b in range(1, B):
             for v in range(VB):
-                if 1 <= b < B - 1 and v < CB // AT_ONCE:
+                if b < B - 1 and v < CB // AT_ONCE:
                     for a in range(AT_ONCE * v, AT_ONCE * (v + 1)):
                         prepare(b + 1, a)
                 if b == B - 1 and v == VB - 1:
                     multiply(b, [v], 0, T // 2)
-                    store(b, v, 0, T // 2)
+                    store(b, v, product[v], 0, T // 2)
                     multiply(b, [v], T // 2, T)
-                    store(b, v, T // 2, T)
+                    store(b, v, product[v], T // 2, T)
                     continue
-                if b > 0 or v >= BANKS:
-                    multiply(b, [v])
-                if b > 0 and v == 0:
-                    norm(b, 1)
-                store(b, v)
+                multiply(b, [v])
+                if v == NORM_AFTER:
+                    norm(b)
+                    for w in range(v):
+                        store(b, w, product[w])
+                if v >= NORM_AFTER:
+                    store(b, v, product[v])
                 if b + 1 < B and v == ADD_UP_AFTER:
                     add_up(b + 1)
+                if b == B - 1:
+                    if v == 0:
+                        add_up(0)
+                    if v == NORM_AFTER + 1:
+                        norm(0)
+                    first = FINISH_AT_ONCE * (v - NORM_AFTER - 2)
+                    for w in range(max(first, 0), min(first + FINISH_AT_ONCE, VB)):
+                        store(0, w, parked[w])

@@ -18,7 +18,6 @@ BANKS = 7
 AT_ONCE = 4
 ADD_UP_AFTER = 2
 NORM_AFTER = 1
-FINISH_AT_ONCE = 2
 
 
 def tile_bitnet_b_kernel(tc, tok_emb, pos_emb, norm_w, head, offs, out):
@@ -145,11 +144,9 @@ def tile_bitnet_b_kernel(tc, tok_emb, pos_emb, norm_w, head, offs, out):
                     store(b, v, product[v])
                 if b + 1 < B and v == ADD_UP_AFTER:
                     add_up(b + 1)
-                if b == B - 1:
-                    if v == 0:
+                    if b + 1 == B - 1:
                         add_up(0)
-                    if v == NORM_AFTER + 1:
-                        norm(0)
-                    first = FINISH_AT_ONCE * (v - NORM_AFTER - 2)
-                    for w in range(max(first, 0), min(first + FINISH_AT_ONCE, VB)):
+                if b == B - 1 and v == 0:
+                    norm(0)
+                    for w in range(VB):
                         store(0, w, parked[w])

@@ -15,9 +15,8 @@ EPS = 1e-6
 FLOPS = 2 * C * S * B * T
 
 BANKS = 7
-AT_ONCE = 4
 ADD_UP_AFTER = 2
-NORM_AFTER = 1
+NORM_AFTER = 2
 
 
 def tile_bitnet_b_kernel(tc, tok_emb, pos_emb, norm_w, head, offs, out):
@@ -120,15 +119,13 @@ def tile_bitnet_b_kernel(tc, tok_emb, pos_emb, norm_w, head, offs, out):
             prepare(1, a)
         multiply(0, range(VB))
 
-        for v in [0, VB - 1] + list(range(1, VB - 1)):
+        early = list(range(NORM_AFTER + 1))
+        for v in early + [VB - 1] + list(range(NORM_AFTER + 1, VB - 1)):
             park(v)
         add_up(1)
 
         for b in range(1, B):
             for v in range(VB):
-                if b < B - 1 and v < CB // AT_ONCE:
-                    for a in range(AT_ONCE * v, AT_ONCE * (v + 1)):
-                        prepare(b + 1, a)
                 if b == B - 1 and v == VB - 1:
                     multiply(b, [v], 0, T // 2)
                     store(b, v, product[v], 0, T // 2)
@@ -138,6 +135,9 @@ def tile_bitnet_b_kernel(tc, tok_emb, pos_emb, norm_w, head, offs, out):
                 multiply(b, [v])
                 if v == NORM_AFTER:
                     norm(b)
+                    if b + 1 < B:
+                        for a in range(CB):
+                            prepare(b + 1, a)
                     for w in range(v):
                         store(b, w, product[w])
                 if v >= NORM_AFTER:

@@ -54,6 +54,7 @@ def tile_bitnet_b_kernel(tc, tok_emb, pos_emb, norm_w, head, offs, out):
         nc.scalar.activation(warm[:], eps[:], ACT.Abs_reciprocal_sqrt)
 
         squares = {}
+        summed = {}
         scaled = {}
         r = {}
         product = {}
@@ -73,15 +74,17 @@ def tile_bitnet_b_kernel(tc, tok_emb, pos_emb, norm_w, head, offs, out):
             nc.scalar.activation(squares[b][:, a, :], h[:], ACT.Square)
 
         def add_up(b):
+            summed[b] = squares[b]
             parts = CB
             while parts > 1:
                 parts //= 2
-                lower = squares[b][:, 0:parts, :]
-                nc.vector.tensor_tensor(lower, lower, squares[b][:, parts : 2 * parts, :], ADD)
+                halved = results.tile([P, parts, T], BF16, name="halved", tag="from_vector")
+                nc.vector.tensor_tensor(halved[:], summed[b][:, 0:parts, :], summed[b][:, parts : 2 * parts, :], ADD)
+                summed[b] = halved
 
         def norm(b):
             total = sums.tile([P, T], F32, name="total")
-            nc.tensor.matmul(total[:], ones[:], squares[b][:, 0, :], start=True, stop=True)
+            nc.tensor.matmul(total[:], ones[:], summed[b][:, 0, :], start=True, stop=True)
             r[b] = held.tile([P, T], F32, name="r%d" % b)
             nc.scalar.activation(r[b][:], total[:], ACT.Abs_reciprocal_sqrt, bias=eps[:], scale=1.0 / C)
 

@@ -16,6 +16,7 @@ FLOPS = 2 * C * S * B * T
 
 BANKS = 7
 ADD_UP_AFTER = 2
+SITS_OUT = 3
 NORM_AFTER = 2
 
 
@@ -44,7 +45,9 @@ def tile_bitnet_b_kernel(tc, tok_emb, pos_emb, norm_w, head, offs, out):
         for a in range(CB):
             nc.sync.dma_start(tok[a][:], tok_blocks[a])
             nc.sync.dma_start(pos[:, a, :], pos_blocks[a])
-            nc.sync.dma_start(head_sb[:, a, :], head_blocks[a])
+            if a > 0:
+                nc.sync.dma_start(head_sb[:, a - 1, :], head_blocks[a - 1])
+        nc.sync.dma_start(head_sb[:, CB - 1, :], head_blocks[CB - 1])
 
         ones = held.tile([P, P], BF16, name="ones")
         nc.vector.memset(ones[:], 1.0)
@@ -119,7 +122,11 @@ def tile_bitnet_b_kernel(tc, tok_emb, pos_emb, norm_w, head, offs, out):
 
         for a in range(CB):
             prepare(0, a)
-            prepare(1, a)
+            if a < SITS_OUT:
+                prepare(1, a)
+            if a > SITS_OUT:
+                prepare(1, a - 1)
+        prepare(1, CB - 1)
         multiply(0, range(VB))
 
         early = list(range(NORM_AFTER + 1))

@@ -76,14 +76,16 @@ def tile_bitnet_b_kernel(tc, tok_emb, pos_emb, norm_w, head, offs, out):
             nc.scalar.activation(scaled[b][:, a, :], h[:], ACT.Identity, scale=gain[:, a : a + 1])
             nc.scalar.activation(squares[b][:, a, :], h[:], ACT.Square)
 
-        def add_up(b):
-            summed[b] = squares[b]
+        def add_up(sequences):
+            for b in sequences:
+                summed[b] = squares[b]
             parts = CB
             while parts > 1:
                 parts //= 2
-                halved = results.tile([P, parts, T], BF16, name="halved", tag="from_vector")
-                nc.vector.tensor_tensor(halved[:], summed[b][:, 0:parts, :], summed[b][:, parts : 2 * parts, :], ADD)
-                summed[b] = halved
+                for b in sequences:
+                    halved = results.tile([P, parts, T], BF16, name="halved", tag="from_vector")
+                    nc.vector.tensor_tensor(halved[:], summed[b][:, 0:parts, :], summed[b][:, parts : 2 * parts, :], ADD)
+                    summed[b] = halved
 
         def norm(b):
             total = sums.tile([P, T], F32, name="total")
@@ -132,7 +134,7 @@ def tile_bitnet_b_kernel(tc, tok_emb, pos_emb, norm_w, head, offs, out):
         early = list(range(NORM_AFTER + 1))
         for v in early + [VB - 1] + list(range(NORM_AFTER + 1, VB - 1)):
             park(v)
-        add_up(1)
+        add_up([1])
 
         for b in range(1, B):
             for v in range(VB):
@@ -152,10 +154,10 @@ def tile_bitnet_b_kernel(tc, tok_emb, pos_emb, norm_w, head, offs, out):
                         store(b, w, product[w])
                 if v >= NORM_AFTER:
                     store(b, v, product[v])
-                if b + 1 < B and v == ADD_UP_AFTER:
-                    add_up(b + 1)
-                    if b + 1 == B - 1:
-                        add_up(0)
+                if b + 1 < B - 1 and v == ADD_UP_AFTER:
+                    add_up([b + 1])
+                if b + 1 == B - 1 and v == ADD_UP_AFTER:
+                    add_up([0, b + 1])
                 if b == B - 1 and v == 0:
                     norm(0)
                     for w in range(VB):

@@ -17,6 +17,7 @@ FLOPS = 2 * C * S * B * T
 BANKS = 7
 ADD_UP_AFTER = 2
 SITS_OUT = 3
+LAST_CUTS = (0, T // 2, 3 * T // 4, T)
 NORM_AFTER = 2
 
 
@@ -139,10 +140,9 @@ def tile_bitnet_b_kernel(tc, tok_emb, pos_emb, norm_w, head, offs, out):
         for b in range(1, B):
             for v in range(VB):
                 if b == B - 1 and v == VB - 1:
-                    multiply(b, [v], 0, T // 2)
-                    store(b, v, product[v], 0, T // 2)
-                    multiply(b, [v], T // 2, T)
-                    store(b, v, product[v], T // 2, T)
+                    for lo, hi in zip(LAST_CUTS[:-1], LAST_CUTS[1:]):
+                        multiply(b, [v], lo, hi)
+                        store(b, v, product[v], lo, hi)
                     continue
                 multiply(b, [v])
                 if v == NORM_AFTER:

@@ -19,6 +19,7 @@ ADD_UP_AFTER = 2
 SITS_OUT = 3
 LAST_CUTS = (0, T // 2, 3 * T // 4, T)
 NORM_AFTER = 2
+FIRST = T // 4
 
 
 def tile_bitnet_b_kernel(tc, tok_emb, pos_emb, norm_w, head, offs, out):
@@ -36,17 +37,21 @@ def tile_bitnet_b_kernel(tc, tok_emb, pos_emb, norm_w, head, offs, out):
         tc.psum_pool(name="products", bufs=BANKS) as products,
     ):
         offsets = held.tile([P, B * T // 16], U16, name="offsets")
-        nc.sync.dma_start(offsets[:], offs)
         gain = held.tile([P, CB], F32, name="gain")
         nc.scalar.dma_start(gain[:], norm_w.rearrange("(p a) o -> p (a o)", a=CB))
 
         tok = [held.tile([P, S], F32, name="tok%d" % a) for a in range(CB)]
         pos = held.tile([P, CB, T], F32, name="pos")
         head_sb = held.tile([P, CB, S], BF16, name="head_sb")
-        for a in range(CB):
+        nc.sync.dma_start(tok[0][:], tok_blocks[0])
+        nc.sync.dma_start(offsets[:], offs)
+        nc.sync.dma_start(pos[:, 0, 0:FIRST], pos_blocks[0][:, 0:FIRST])
+        nc.sync.dma_start(head_sb[:, 0, :], head_blocks[0])
+        nc.sync.dma_start(pos[:, 0, FIRST:T], pos_blocks[0][:, FIRST:T])
+        for a in range(1, CB):
             nc.sync.dma_start(tok[a][:], tok_blocks[a])
             nc.sync.dma_start(pos[:, a, :], pos_blocks[a])
-            if a > 0:
+            if a > 1:
                 nc.sync.dma_start(head_sb[:, a - 1, :], head_blocks[a - 1])
         nc.sync.dma_start(head_sb[:, CB - 1, :], head_blocks[CB - 1])
 
@@ -64,18 +69,18 @@ def tile_bitnet_b_kernel(tc, tok_emb, pos_emb, norm_w, head, offs, out):
         product = {}
         parked = {}
 
-        def prepare(b, a):
-            if a == 0:
+        def prepare(b, a, lo=0, hi=T):
+            if a == 0 and lo == 0:
                 if b == 0:
                     squares[b] = held.tile([P, CB, T], BF16, name="squares_kept")
                 else:
                     squares[b] = operands.tile([P, CB, T], BF16, name="squares")
                 scaled[b] = operands.tile([P, CB, T], BF16, name="scaled")
-            piece = offsets[:, b * (T // 16) : (b + 1) * (T // 16)]
-            h = results.tile([P, T], F32, name="h", tag="from_vector")
-            nc.vector.tensor_tensor(h[:], tok[a][:].indirect(piece), pos[:, a, :], ADD)
-            nc.scalar.activation(scaled[b][:, a, :], h[:], ACT.Identity, scale=gain[:, a : a + 1])
-            nc.scalar.activation(squares[b][:, a, :], h[:], ACT.Square)
+            piece = offsets[:, (b * T + lo) // 16 : (b * T + hi) // 16]
+            h = results.tile([P, hi - lo], F32, name="h", tag="from_vector")
+            nc.vector.tensor_tensor(h[:], tok[a][:].indirect(piece), pos[:, a, lo:hi], ADD)
+            nc.scalar.activation(scaled[b][:, a, lo:hi], h[:], ACT.Identity, scale=gain[:, a : a + 1])
+            nc.scalar.activation(squares[b][:, a, lo:hi], h[:], ACT.Square)
 
         def add_up(sequences):
             for b in sequences:
@@ -101,14 +106,16 @@ def tile_bitnet_b_kernel(tc, tok_emb, pos_emb, norm_w, head, offs, out):
                 else:
                     product[v] = sums.tile([P, hi - lo], F32, name="total")
             for a in range(CB):
-                for v in words:
-                    nc.tensor.matmul(
-                        product[v][:],
-                        head_sb[:, a, v * P : (v + 1) * P],
-                        scaled[b][:, a, lo:hi],
-                        start=(a == 0),
-                        stop=(a == CB - 1),
-                    )
+                cuts = (lo, FIRST, hi) if (b == 0 and a == 0) else (lo, hi)
+                for left, right in zip(cuts[:-1], cuts[1:]):
+                    for v in words:
+                        nc.tensor.matmul(
+                            product[v][:, left - lo : right - lo],
+                            head_sb[:, a, v * P : (v + 1) * P],
+                            scaled[b][:, a, left:right],
+                            start=(a == 0 and left == lo),
+                            stop=(a == CB - 1),
+                        )
 
         def park(v):
             if v == 0:
@@ -124,7 +131,11 @@ def tile_bitnet_b_kernel(tc, tok_emb, pos_emb, norm_w, head, offs, out):
             nc.sync.dma_start(out[v * P : (v + 1) * P, b * T + lo : b * T + hi], logits[:])
 
         for a in range(CB):
-            prepare(0, a)
+            if a == 0:
+                prepare(0, a, 0, FIRST)
+                prepare(0, a, FIRST, T)
+            else:
+                prepare(0, a)
             if a < SITS_OUT:
                 prepare(1, a)
             if a > SITS_OUT:

import concourse.mybir as mybir

F32 = mybir.dt.float32
BF16 = mybir.dt.bfloat16
U16 = mybir.dt.uint16
ADD = mybir.AluOpType.add
MULT = mybir.AluOpType.mult
ACT = mybir.ActivationFunctionType

P = 128
C, S, B, T = 1024, 1024, 4, 512
CB = C // P
VB = S // P
EPS = 1e-6
FLOPS = 2 * C * S * B * T

BANKS = 7
ADD_UP_AFTER = 2
SITS_OUT = 3
LAST_CUTS = (0, T // 2, 3 * T // 4, T)
NORM_AFTER = 2
FIRST = T // 4


def tile_bitnet_b_kernel(tc, tok_emb, pos_emb, norm_w, head, offs, out):
    nc = tc.nc

    tok_blocks = tok_emb.rearrange("(p a) s -> a p s", a=CB)
    pos_blocks = pos_emb.rearrange("(p a) t -> a p t", a=CB)
    head_blocks = head.rearrange("(p a) v -> a p v", a=CB)

    with (
        tc.tile_pool(name="held", bufs=1) as held,
        tc.tile_pool(name="operands", bufs=2) as operands,
        tc.tile_pool(name="results", bufs=12) as results,
        tc.psum_pool(name="sums", bufs=1) as sums,
        tc.psum_pool(name="products", bufs=BANKS) as products,
    ):
        offsets = held.tile([P, B * T // 16], U16, name="offsets")
        gain = held.tile([P, CB], F32, name="gain")
        nc.scalar.dma_start(gain[:], norm_w.rearrange("(p a) o -> p (a o)", a=CB))

        tok = [held.tile([P, S], F32, name="tok%d" % a) for a in range(CB)]
        pos = held.tile([P, CB, T], F32, name="pos")
        head_sb = held.tile([P, CB, S], BF16, name="head_sb")
        nc.sync.dma_start(tok[0][:], tok_blocks[0])
        nc.sync.dma_start(offsets[:], offs)
        nc.sync.dma_start(pos[:, 0, 0:FIRST], pos_blocks[0][:, 0:FIRST])
        nc.sync.dma_start(head_sb[:, 0, :], head_blocks[0])
        nc.sync.dma_start(pos[:, 0, FIRST:T], pos_blocks[0][:, FIRST:T])
        for a in range(1, CB):
            nc.sync.dma_start(tok[a][:], tok_blocks[a])
            nc.sync.dma_start(pos[:, a, :], pos_blocks[a])
            if a > 1:
                nc.sync.dma_start(head_sb[:, a - 1, :], head_blocks[a - 1])
        nc.sync.dma_start(head_sb[:, CB - 1, :], head_blocks[CB - 1])

        ones = held.tile([P, P], BF16, name="ones")
        nc.vector.memset(ones[:], 1.0)
        eps = held.tile([P, 1], F32, name="eps")
        nc.vector.memset(eps[:], EPS)
        warm = held.tile([P, 1], F32, name="warm")
        nc.scalar.activation(warm[:], eps[:], ACT.Abs_reciprocal_sqrt)

        squares = {}
        summed = {}
        scaled = {}
        r = {}
        product = {}
        parked = {}

        def prepare(b, a, lo=0, hi=T):
            if a == 0 and lo == 0:
                if b == 0:
                    squares[b] = held.tile([P, CB, T], BF16, name="squares_kept")
                else:
                    squares[b] = operands.tile([P, CB, T], BF16, name="squares")
                scaled[b] = operands.tile([P, CB, T], BF16, name="scaled")
            piece = offsets[:, (b * T + lo) // 16 : (b * T + hi) // 16]
            h = results.tile([P, hi - lo], F32, name="h", tag="from_vector")
            nc.vector.tensor_tensor(h[:], tok[a][:].indirect(piece), pos[:, a, lo:hi], ADD)
            nc.scalar.activation(scaled[b][:, a, lo:hi], h[:], ACT.Identity, scale=gain[:, a : a + 1])
            nc.scalar.activation(squares[b][:, a, lo:hi], h[:], ACT.Square)

        def add_up(sequences):
            for b in sequences:
                summed[b] = squares[b]
            parts = CB
            while parts > 1:
                parts //= 2
                for b in sequences:
                    halved = results.tile([P, parts, T], BF16, name="halved", tag="from_vector")
                    nc.vector.tensor_tensor(halved[:], summed[b][:, 0:parts, :], summed[b][:, parts : 2 * parts, :], ADD)
                    summed[b] = halved

        def norm(b):
            total = sums.tile([P, T], F32, name="total")
            nc.tensor.matmul(total[:], ones[:], summed[b][:, 0, :], start=True, stop=True)
            r[b] = held.tile([P, T], F32, name="r%d" % b)
            nc.scalar.activation(r[b][:], total[:], ACT.Abs_reciprocal_sqrt, bias=eps[:], scale=1.0 / C)

        def multiply(b, words, lo=0, hi=T):
            for v in words:
                if v < BANKS or b > 0:
                    product[v] = products.tile([P, hi - lo], F32, name="product")
                else:
                    product[v] = sums.tile([P, hi - lo], F32, name="total")
            for a in range(CB):
                cuts = (lo, FIRST, hi) if (b == 0 and a == 0) else (lo, hi)
                for left, right in zip(cuts[:-1], cuts[1:]):
                    for v in words:
                        nc.tensor.matmul(
                            product[v][:, left - lo : right - lo],
                            head_sb[:, a, v * P : (v + 1) * P],
                            scaled[b][:, a, left:right],
                            start=(a == 0 and left == lo),
                            stop=(a == CB - 1),
                        )

        def park(v):
            if v == 0:
                parked[v] = results.tile([P, T], F32, name="moved", tag="from_vector")
                nc.vector.tensor_copy(parked[v][:], product[v][:])
            else:
                parked[v] = held.tile([P, T], F32, name="parked%d" % v)
                nc.scalar.copy(parked[v][:], product[v][:])

        def store(b, v, source, lo=0, hi=T):
            logits = results.tile([P, hi - lo], F32, name="logits", tag="from_vector")
            nc.vector.tensor_tensor(logits[:], source[:], r[b][:, lo:hi], MULT)
            nc.sync.dma_start(out[v * P : (v + 1) * P, b * T + lo : b * T + hi], logits[:])

        for a in range(CB):
            if a == 0:
                prepare(0, a, 0, FIRST)
                prepare(0, a, FIRST, T)
            else:
                prepare(0, a)
            if a < SITS_OUT:
                prepare(1, a)
            if a > SITS_OUT:
                prepare(1, a - 1)
        prepare(1, CB - 1)
        multiply(0, range(VB))

        early = list(range(NORM_AFTER + 1))
        for v in early + [VB - 1] + list(range(NORM_AFTER + 1, VB - 1)):
            park(v)
        add_up([1])

        for b in range(1, B):
            for v in range(VB):
                if b == B - 1 and v == VB - 1:
                    for lo, hi in zip(LAST_CUTS[:-1], LAST_CUTS[1:]):
                        multiply(b, [v], lo, hi)
                        store(b, v, product[v], lo, hi)
                    continue
                multiply(b, [v])
                if v == NORM_AFTER:
                    norm(b)
                    if b + 1 < B:
                        for a in range(CB):
                            prepare(b + 1, a)
                    for w in range(v):
                        store(b, w, product[w])
                if v >= NORM_AFTER:
                    store(b, v, product[v])
                if b + 1 < B - 1 and v == ADD_UP_AFTER:
                    add_up([b + 1])
                if b + 1 == B - 1 and v == ADD_UP_AFTER:
                    add_up([0, b + 1])
                if b == B - 1 and v == 0:
                    norm(0)
                    for w in range(VB):
                        store(0, w, parked[w])
